import numpy as np
import ml_dtypes


def mxq(x, axis, fmt="e4m3"):
    dtype, down = {"e4m3": (ml_dtypes.float8_e4m3fn, 7), "e5m2": (ml_dtypes.float8_e5m2, 14)}[fmt]
    v = np.moveaxis(np.asarray(x, np.float32).astype(ml_dtypes.bfloat16).astype(np.float64), axis, -1)
    blocks = v.reshape(v.shape[:-1] + (-1, 32))
    amax = np.abs(blocks).max(-1, keepdims=True)
    byte = np.maximum(np.where(amax > 0, np.frexp(amax)[1] - 1 + 127, 0) - down, 1)
    scale = np.exp2(byte - 127.0)
    codes = (blocks / scale).astype(np.float32).astype(dtype).astype(np.float64)
    return np.moveaxis((codes * scale).reshape(v.shape), -1, axis)


WIDE = False


def mx_kscale(k):
    if not WIDE:
        return np.ones(k)
    levels = np.array([10, -10, 5, -5, 0])
    a = np.random.permutation(np.resize(levels, k // 512 * 4)).reshape(k // 512, 4)
    idx = np.arange(k)
    return np.exp2(a[idx // 512, idx % 128 // 32])


BF16 = ml_dtypes.bfloat16


def bf(x):
    return np.asarray(x, np.float32).astype(BF16)


def f64(x):
    return np.asarray(x).astype(np.float64)


E2M1 = np.array([0.0, 0.5, 1.0, 1.5, 2.0, 3.0, 4.0, 6.0, -0.0, -0.5, -1.0, -1.5, -2.0, -3.0, -4.0, -6.0])


def pack_weight(w, fmt):
    k, n = w.shape
    w = f64(bf(w)).reshape(k // 32, 32, n)
    amax = np.abs(w).max(1)
    if fmt == "e4m3":
        byte = np.frexp(amax)[1] - 1 + 127 - 7
    else:
        mant, ex = np.frexp(amax / 6.0)
        byte = np.where(mant > 0.5, ex, ex - 1) + 127
    byte = np.clip(np.where(amax > 0, byte, 1), 1, 254)
    scaled = (w * np.exp2(127.0 - byte)[:, None, :]).reshape(k, n).astype(np.float32)
    by_word = np.ascontiguousarray(scaled.reshape(k // 512, 128, 4, n).transpose(0, 1, 3, 2))
    if fmt == "e4m3":
        words = by_word.astype(ml_dtypes.float8_e4m3fn).view(np.uint8)
    else:
        c = by_word.astype(ml_dtypes.float4_e2m1fn).view(np.uint8) & 0xF
        words = c[..., 0::2] | (c[..., 1::2] << 4)
    return np.ascontiguousarray(words), np.ascontiguousarray(byte.astype(np.uint8).reshape(k // 512, 16, n))


def unpack_weight(words, scales, fmt):
    g, p, n, _ = words.shape
    if fmt == "e4m3":
        vals = np.ascontiguousarray(words).view(ml_dtypes.float8_e4m3fn).astype(np.float64)
    else:
        nib = np.empty((g, p, n, 4), np.uint8)
        nib[..., 0::2] = words & 0xF
        nib[..., 1::2] = words >> 4
        vals = E2M1[nib]
    vals = vals * np.repeat(np.exp2(scales.astype(np.float64) - 127.0), 8, axis=1)[..., None]
    return vals.transpose(0, 1, 3, 2).reshape(g * 512, n)


B, EN_MID, DE_MID = 128, 8192, 6144
K1 = EN_MID // 2
K2 = DE_MID // 2


def setup_inputs():
    s = mx_kscale(K1)
    in_data = np.random.standard_normal((B, K1, 2)) * s[None, :, None]
    w = np.random.standard_normal((DE_MID, K1)) / np.sqrt(K1) / s[None, :]
    W_words, W_scales = pack_weight(w.T, "e4m3")
    return {"in_data": bf(in_data.reshape(B, EN_MID)),
            "W_words": W_words,
            "W_scales": W_scales,
            "bias": bf(np.random.standard_normal(DE_MID) * 0.25)}


def reference(in_data, W_words, W_scales, bias):
    Bsz = in_data.shape[0]
    x_imag = f64(in_data).reshape(Bsz, K1, 2)[:, :, 1]
    tmp = mxq(x_imag, 1, "e4m3") @ unpack_weight(W_words, W_scales, "e4m3")
    act = np.maximum(tmp + f64(bias), 0.0)
    out_r = act[:, :K2] - act[:, K2:]
    out = np.stack([out_r, np.zeros_like(out_r)], axis=2)
    return out.reshape(Bsz, DE_MID, 1)

@@ -1,0 +1,177 @@
+import concourse.mybir as mybir
+from concourse.masks import make_identity
+
+F32 = mybir.dt.float32
+BF16 = mybir.dt.bfloat16
+I32 = mybir.dt.int32
+U32 = mybir.dt.uint32
+U8 = mybir.dt.uint8
+FP8X4 = mybir.dt.float8_e4m3fn_x4
+ALU = mybir.AluOpType
+ACT = mybir.ActivationFunctionType
+
+P = 128
+B = 128
+K = 4096
+G = K // 512
+N = 6144
+H = N // 2
+BANK = 512
+HB = H // BANK
+
+FLOPS = 2 * B * K * N
+
+ROUNDS = ((0, 6, 1), (6, 3, 1), (9, 2, 1), (11, 1, 2))
+W_BUFS = 10
+AHEAD = W_BUFS - 1
+
+
+def tile_middlelayer_w_kernel(tc, in_data, W_words, W_scales, bias, out):
+    nc = tc.nc
+    out_rows = out.rearrange("b n o -> b (n o)")
+    bias_by_bank = bias.rearrange("(r c) -> r c", c=BANK)
+
+    with tc.tile_pool(name="keep", bufs=1) as keep, tc.tile_pool(name="wpool", bufs=W_BUFS) as wpool, tc.tile_pool(
+        name="tmp", bufs=3
+    ) as tmp, tc.psum_pool(name="psum", bufs=8) as psum:
+        planes = [keep.tile([P, 2, H], U8, name="planes%d" % s, align_bytes=64) for s in range(2)]
+        bias_rows = keep.tile([P, BANK], BF16, name="bias_rows")
+        out_sb = keep.tile([P, H, 2], F32, name="out_sb")
+        nc.vector.memset(planes[0][:].bitcast(I32), 0)
+        nc.vector.memset(bias_rows[:], 0.0)
+        nc.vector.memset(planes[1][:].bitcast(I32), 0)
+        nc.vector.memset(out_sb[:], 0.0)
+
+        ident_f = keep.tile([P, P], F32, name="ident_f")
+        make_identity(nc, ident_f[:])
+        ident_b = keep.tile([P, P], BF16, name="ident_b")
+        make_identity(nc, ident_b[:])
+
+        x_raw = keep.tile([P, 2 * K], BF16, name="x_raw")
+        for i in range(4):
+            nc.sync.dma_start(out=x_raw[:, 2048 * i : 2048 * (i + 1)], in_=in_data[:, 2048 * i : 2048 * (i + 1)])
+        nc.scalar.dma_start(out=bias_rows[0:8, :], in_=bias_by_bank[0:8, :])
+        nc.scalar.dma_start(out=bias_rows[8:12, :], in_=bias_by_bank[8:12, :])
+
+        def load_scales(s):
+            for h in range(2):
+                for q in range(4):
+                    nc.sync.dma_start(
+                        out=planes[s][32 * q : 32 * q + 16, h, :].bitcast(I32),
+                        in_=W_scales[4 * h : 4 * h + 4, 4 * q : 4 * q + 4, H * s : H * (s + 1)].bitcast(I32),
+                    )
+
+        load_scales(0)
+
+        chunks = []
+        for r, (c0, nb, gs) in enumerate(ROUNDS):
+            for g0 in range(0, G, gs):
+                chunks.append((r, g0, gs))
+        w_tiles = {}
+
+        def load_w(i):
+            if i >= len(chunks):
+                return
+            r, g0, gs = chunks[i]
+            c0, nb, gs2 = ROUNDS[r]
+            if r == 1 and g0 == 0:
+                load_scales(1)
+            w = wpool.tile([P, gs, nb * BANK], U32, tag="w", name="w", align_bytes=64)
+            src = W_words[g0 : g0 + gs].rearrange("g p n t -> p g (n t)")
+            nc.sync.dma_start(
+                out=w[:].bitcast(I32),
+                in_=src[:, :, 4 * BANK * c0 : 4 * BANK * (c0 + nb)].bitcast(I32),
+            )
+            w_tiles[i] = w
+
+        for i in range(AHEAD):
+            load_w(i)
+
+        x_sorted = keep.tile([P, G, 2, P], F32, name="x_sorted")
+        src_x = x_raw[:].rearrange("b (g p u e c) -> b g u p e c", g=G, p=P, u=2, e=2, c=2)
+        dst_x = x_sorted[:].bitcast(BF16).rearrange("b g u (p e) -> b g u p e", e=2)
+        for g in range(G):
+            if g % 2 == 0:
+                nc.vector.tensor_copy(out=dst_x[:, g, :, :, :], in_=src_x[:, g, :, :, :, 1])
+            else:
+                nc.scalar.copy(out=dst_x[:, g, :, :, :], in_=src_x[:, g, :, :, :, 1])
+
+        grouped = keep.tile([P, G, 4 * B], BF16, name="grouped", align_bytes=64)
+        grouped_w = grouped[:].bitcast(F32).rearrange("p g (b u) -> p g b u", u=2)
+        x_codes = keep.tile([P, G * B], U32, name="x_codes", align_bytes=64)
+        x_planes = keep.tile([P, G * B], U8, name="x_planes", align_bytes=64)
+        for i in range(4):
+            xt = psum.tile([P, 2, 2, B], F32, tag="bank", name="xt")
+            for gg in range(2):
+                for u in range(2):
+                    nc.tensor.transpose(xt[:, gg, u, :], x_sorted[:, 2 * i + gg, u, :], ident_f[:])
+            if i % 2 == 0:
+                nc.vector.tensor_copy(out=grouped_w[:, 2 * i : 2 * i + 2, :, :], in_=xt[:].rearrange("p g u b -> p g b u"))
+            else:
+                nc.scalar.copy(out=grouped_w[:, 2 * i : 2 * i + 2, :, :], in_=xt[:].rearrange("p g u b -> p g b u"))
+        for i in range(4):
+            nc.vector.quantize_mx(
+                out=x_codes[:, 2 * B * i : 2 * B * (i + 1)].bitcast(FP8X4),
+                scales=x_planes[:, 2 * B * i : 2 * B * (i + 1)],
+                in_=grouped[:, 2 * i : 2 * i + 2, :].rearrange("p g c -> p (g c)"),
+            )
+
+        bias_bc = keep.tile([P, N], BF16, name="bias_bc")
+        for i in range(N // (2 * BANK)):
+            bb = psum.tile([P, 2 * BANK], BF16, tag="bank", name="bb")
+            for s in range(2):
+                c = 2 * i + s
+                nc.tensor.matmul(
+                    bb[:, BANK * s : BANK * (s + 1)],
+                    lhsT=ident_b[:, c : c + 1].to_broadcast([P, P]),
+                    rhs=bias_rows[:],
+                    start=True,
+                    stop=True,
+                )
+            nc.scalar.copy(out=bias_bc[:, 2 * BANK * i : 2 * BANK * (i + 1)], in_=bb[:])
+
+        a1 = keep.tile([P, H], F32, name="a1")
+        i = 0
+        for r, (c0, nb, gs) in enumerate(ROUNDS):
+            accs = [psum.tile([P, BANK], F32, tag="bank", name="acc%d" % (c0 + j)) for j in range(nb)]
+            for g0 in range(0, G, gs):
+                load_w(i + AHEAD)
+                w = w_tiles[i]
+                i += 1
+                for gi in range(gs):
+                    g = g0 + gi
+                    for j in range(nb):
+                        s, cc = divmod(c0 + j, HB)
+                        nc.tensor.matmul_mx(
+                            out=accs[j][:],
+                            lhsT=x_codes[:, B * g : B * (g + 1)].bitcast(FP8X4),
+                            lhsT_scale=x_planes[:, B * g : B * (g + 1)],
+                            rhs=w[:, gi, BANK * j : BANK * (j + 1)].bitcast(FP8X4),
+                            rhs_scale=planes[s][4 * (g % 4) : P, g // 4, BANK * cc : BANK * (cc + 1)],
+                            start=(g == 0),
+                            stop=(g == G - 1),
+                        )
+            for j in range(nb):
+                c = c0 + j
+                cols = slice(BANK * c, BANK * (c + 1))
+                if c < HB:
+                    nc.vector.tensor_tensor(out=a1[:, cols], in0=accs[j][:], in1=bias_bc[:, cols], op=ALU.add)
+                    nc.scalar.activation(out=a1[:, cols], in_=a1[:, cols], func=ACT.Relu)
+                else:
+                    j0 = BANK * (c - HB)
+                    nt = tmp.tile([P, BANK], F32, name="nt")
+                    nc.vector.scalar_tensor_tensor(
+                        out=nt[:], in0=accs[j][:], scalar=-1.0, in1=bias_bc[:, cols], op0=ALU.mult, op1=ALU.subtract
+                    )
+                    nc.vector.scalar_tensor_tensor(
+                        out=out_sb[:, j0 : j0 + BANK, 0],
+                        in0=nt[:],
+                        scalar=0.0,
+                        in1=a1[:, j0 : j0 + BANK],
+                        op0=ALU.min,
+                        op1=ALU.add,
+                    )
+                    nc.sync.dma_start(
+                        out=out_rows[:, 2 * j0 : 2 * (j0 + BANK)],
+                        in_=out_sb[:, j0 : j0 + BANK, :].rearrange("p j e -> p (j e)"),
+                    )

@@ -33,23 +33,22 @@ def tile_middlelayer_w_kernel(tc, in_data, W_words, W_scales, bias, out):
 
     with tc.tile_pool(name="keep", bufs=1) as keep, tc.tile_pool(name="wpool", bufs=W_BUFS) as wpool, tc.tile_pool(
         name="tmp", bufs=3
-    ) as tmp, tc.psum_pool(name="psum", bufs=8) as psum:
+    ) as tmp, tc.psum_pool(name="psum", bufs=8) as psum, tc.manual_schedule():
         planes = [keep.tile([P, 2, H], U8, name="planes%d" % s, align_bytes=64) for s in range(2)]
         bias_rows = keep.tile([P, BANK], BF16, name="bias_rows")
         out_sb = keep.tile([P, H, 2], F32, name="out_sb")
-        nc.vector.memset(planes[0][:].bitcast(I32), 0)
         nc.vector.memset(bias_rows[:], 0.0)
+        nc.vector.memset(planes[0][:].bitcast(I32), 0)
         nc.vector.memset(planes[1][:].bitcast(I32), 0)
-        nc.vector.memset(out_sb[:], 0.0)
 
-        ident_f = keep.tile([P, P], F32, name="ident_f")
-        make_identity(nc, ident_f[:])
         ident_b = keep.tile([P, P], BF16, name="ident_b")
         make_identity(nc, ident_b[:])
+        ident_f = keep.tile([P, P], F32, name="ident_f")
+        make_identity(nc, ident_f[:])
 
         x_raw = keep.tile([P, 2 * K], BF16, name="x_raw")
-        for i in range(4):
-            nc.sync.dma_start(out=x_raw[:, 2048 * i : 2048 * (i + 1)], in_=in_data[:, 2048 * i : 2048 * (i + 1)])
+        for i in range(2):
+            nc.sync.dma_start(out=x_raw[:, K * i : K * (i + 1)], in_=in_data[:, K * i : K * (i + 1)])
         nc.scalar.dma_start(out=bias_rows[0:8, :], in_=bias_by_bank[0:8, :])
         nc.scalar.dma_start(out=bias_rows[8:12, :], in_=bias_by_bank[8:12, :])
 
@@ -87,36 +86,8 @@ def tile_middlelayer_w_kernel(tc, in_data, W_words, W_scales, bias, out):
         for i in range(AHEAD):
             load_w(i)
 
-        x_sorted = keep.tile([P, G, 2, P], F32, name="x_sorted")
-        src_x = x_raw[:].rearrange("b (g p u e c) -> b g u p e c", g=G, p=P, u=2, e=2, c=2)
-        dst_x = x_sorted[:].bitcast(BF16).rearrange("b g u (p e) -> b g u p e", e=2)
-        for g in range(G):
-            if g % 2 == 0:
-                nc.vector.tensor_copy(out=dst_x[:, g, :, :, :], in_=src_x[:, g, :, :, :, 1])
-            else:
-                nc.scalar.copy(out=dst_x[:, g, :, :, :], in_=src_x[:, g, :, :, :, 1])
-
-        grouped = keep.tile([P, G, 4 * B], BF16, name="grouped", align_bytes=64)
-        grouped_w = grouped[:].bitcast(F32).rearrange("p g (b u) -> p g b u", u=2)
-        x_codes = keep.tile([P, G * B], U32, name="x_codes", align_bytes=64)
-        x_planes = keep.tile([P, G * B], U8, name="x_planes", align_bytes=64)
-        for i in range(4):
-            xt = psum.tile([P, 2, 2, B], F32, tag="bank", name="xt")
-            for gg in range(2):
-                for u in range(2):
-                    nc.tensor.transpose(xt[:, gg, u, :], x_sorted[:, 2 * i + gg, u, :], ident_f[:])
-            if i % 2 == 0:
-                nc.vector.tensor_copy(out=grouped_w[:, 2 * i : 2 * i + 2, :, :], in_=xt[:].rearrange("p g u b -> p g b u"))
-            else:
-                nc.scalar.copy(out=grouped_w[:, 2 * i : 2 * i + 2, :, :], in_=xt[:].rearrange("p g u b -> p g b u"))
-        for i in range(4):
-            nc.vector.quantize_mx(
-                out=x_codes[:, 2 * B * i : 2 * B * (i + 1)].bitcast(FP8X4),
-                scales=x_planes[:, 2 * B * i : 2 * B * (i + 1)],
-                in_=grouped[:, 2 * i : 2 * i + 2, :].rearrange("p g c -> p (g c)"),
-            )
-
         bias_bc = keep.tile([P, N], BF16, name="bias_bc")
+        bbs = []
         for i in range(N // (2 * BANK)):
             bb = psum.tile([P, 2 * BANK], BF16, tag="bank", name="bb")
             for s in range(2):
@@ -128,9 +99,39 @@ def tile_middlelayer_w_kernel(tc, in_data, W_words, W_scales, bias, out):
                     start=True,
                     stop=True,
                 )
+            bbs.append(bb)
+
+        x_sorted = keep.tile([P, G, 2, P], F32, name="x_sorted")
+        src_x = x_raw[:].rearrange("b (g p u e c) -> b g u p e c", g=G, p=P, u=2, e=2, c=2)
+        dst_x = x_sorted[:].bitcast(BF16).rearrange("b g u (p e) -> b g u p e", e=2)
+        for g in range(G):
+            if g % 2 == 0:
+                nc.vector.tensor_copy(out=dst_x[:, g, :, :, :], in_=src_x[:, g, :, :, :, 1])
+            else:
+                nc.scalar.copy(out=dst_x[:, g, :, :, :], in_=src_x[:, g, :, :, :, 1])
+        for i, bb in enumerate(bbs):
             nc.scalar.copy(out=bias_bc[:, 2 * BANK * i : 2 * BANK * (i + 1)], in_=bb[:])
 
+        grouped = keep.tile([P, G, 4 * B], BF16, name="grouped", align_bytes=64)
+        grouped_w = grouped[:].bitcast(F32).rearrange("p g (b u) -> p g b u", u=2)
+        x_codes = keep.tile([P, G * B], U32, name="x_codes", align_bytes=64)
+        x_planes = keep.tile([P, G * B], U8, name="x_planes", align_bytes=64)
+        for i in range(4):
+            xt = psum.tile([P, 2, 2, B], F32, tag="bank", name="xt")
+            for gg in range(2):
+                for u in range(2):
+                    nc.tensor.transpose(xt[:, gg, u, :], x_sorted[:, 2 * i + gg, u, :], ident_f[:])
+            nc.vector.tensor_copy(out=grouped_w[:, 2 * i : 2 * i + 2, :, :], in_=xt[:].rearrange("p g u b -> p g b u"))
+        for i in range(4):
+            nc.vector.quantize_mx(
+                out=x_codes[:, 2 * B * i : 2 * B * (i + 1)].bitcast(FP8X4),
+                scales=x_planes[:, 2 * B * i : 2 * B * (i + 1)],
+                in_=grouped[:, 2 * i : 2 * i + 2, :].rearrange("p g c -> p (g c)"),
+            )
+        nc.vector.memset(out_sb[:], 0.0)
+
         a1 = keep.tile([P, H], F32, name="a1")
+        pending = []
         i = 0
         for r, (c0, nb, gs) in enumerate(ROUNDS):
             accs = [psum.tile([P, BANK], F32, tag="bank", name="acc%d" % (c0 + j)) for j in range(nb)]
@@ -171,7 +172,11 @@ def tile_middlelayer_w_kernel(tc, in_data, W_words, W_scales, bias, out):
                         op0=ALU.min,
                         op1=ALU.add,
                     )
-                    nc.sync.dma_start(
-                        out=out_rows[:, 2 * j0 : 2 * (j0 + BANK)],
-                        in_=out_sb[:, j0 : j0 + BANK, :].rearrange("p j e -> p (j e)"),
-                    )
+                    pending.append(j0)
+                    if i + AHEAD >= len(chunks):
+                        for js in pending:
+                            nc.sync.dma_start(
+                                out=out_rows[:, 2 * js : 2 * (js + BANK)],
+                                in_=out_sb[:, js : js + BANK, :].rearrange("p j e -> p (j e)"),
+                            )
+                        pending = []

@@ -34,12 +34,12 @@ def tile_middlelayer_w_kernel(tc, in_data, W_words, W_scales, bias, out):
     with tc.tile_pool(name="keep", bufs=1) as keep, tc.tile_pool(name="wpool", bufs=W_BUFS) as wpool, tc.tile_pool(
         name="tmp", bufs=3
     ) as tmp, tc.psum_pool(name="psum", bufs=8) as psum, tc.manual_schedule():
-        planes = [keep.tile([P, 2, H], U8, name="planes%d" % s, align_bytes=64) for s in range(2)]
+        planes = keep.tile([P, 2, N], U8, name="planes", align_bytes=64)
         bias_rows = keep.tile([P, BANK], BF16, name="bias_rows")
         out_sb = keep.tile([P, H, 2], F32, name="out_sb")
+        nc.vector.memset(planes[:, 0, :].bitcast(I32), 0)
+        nc.vector.memset(planes[:, 1, :].bitcast(I32), 0)
         nc.vector.memset(bias_rows[:], 0.0)
-        nc.vector.memset(planes[0][:].bitcast(I32), 0)
-        nc.vector.memset(planes[1][:].bitcast(I32), 0)
 
         ident_b = keep.tile([P, P], BF16, name="ident_b")
         make_identity(nc, ident_b[:])
@@ -52,15 +52,12 @@ def tile_middlelayer_w_kernel(tc, in_data, W_words, W_scales, bias, out):
         nc.scalar.dma_start(out=bias_rows[0:8, :], in_=bias_by_bank[0:8, :])
         nc.scalar.dma_start(out=bias_rows[8:12, :], in_=bias_by_bank[8:12, :])
 
-        def load_scales(s):
-            for h in range(2):
-                for q in range(4):
-                    nc.sync.dma_start(
-                        out=planes[s][32 * q : 32 * q + 16, h, :].bitcast(I32),
-                        in_=W_scales[4 * h : 4 * h + 4, 4 * q : 4 * q + 4, H * s : H * (s + 1)].bitcast(I32),
-                    )
-
-        load_scales(0)
+        for h in range(2):
+            for q in (0, 2, 1, 3):
+                nc.gpsimd.dma_start(
+                    out=planes[32 * q : 32 * q + 16, h, :].bitcast(F32),
+                    in_=W_scales[4 * h : 4 * h + 4, 4 * q : 4 * q + 4, :].bitcast(F32),
+                )
 
         chunks = []
         for r, (c0, nb, gs) in enumerate(ROUNDS):
@@ -73,8 +70,6 @@ def tile_middlelayer_w_kernel(tc, in_data, W_words, W_scales, bias, out):
                 return
             r, g0, gs = chunks[i]
             c0, nb, gs2 = ROUNDS[r]
-            if r == 1 and g0 == 0:
-                load_scales(1)
             w = wpool.tile([P, gs, nb * BANK], U32, tag="w", name="w", align_bytes=64)
             src = W_words[g0 : g0 + gs].rearrange("g p n t -> p g (n t)")
             nc.sync.dma_start(
@@ -142,13 +137,13 @@ def tile_middlelayer_w_kernel(tc, in_data, W_words, W_scales, bias, out):
                 for gi in range(gs):
                     g = g0 + gi
                     for j in range(nb):
-                        s, cc = divmod(c0 + j, HB)
+                        c = c0 + j
                         nc.tensor.matmul_mx(
                             out=accs[j][:],
                             lhsT=x_codes[:, B * g : B * (g + 1)].bitcast(FP8X4),
                             lhsT_scale=x_planes[:, B * g : B * (g + 1)],
                             rhs=w[:, gi, BANK * j : BANK * (j + 1)].bitcast(FP8X4),
-                            rhs_scale=planes[s][4 * (g % 4) : P, g // 4, BANK * cc : BANK * (cc + 1)],
+                            rhs_scale=planes[4 * (g % 4) : P, g // 4, BANK * c : BANK * (c + 1)],
                             start=(g == 0),
                             stop=(g == G - 1),
                         )

@@ -37,9 +37,9 @@ def tile_middlelayer_w_kernel(tc, in_data, W_words, W_scales, bias, out):
         planes = keep.tile([P, 2, N], U8, name="planes", align_bytes=64)
         bias_rows = keep.tile([P, BANK], BF16, name="bias_rows")
         out_sb = keep.tile([P, H, 2], F32, name="out_sb")
+        nc.vector.memset(bias_rows[:], 0.0)
         nc.vector.memset(planes[:, 0, :].bitcast(I32), 0)
         nc.vector.memset(planes[:, 1, :].bitcast(I32), 0)
-        nc.vector.memset(bias_rows[:], 0.0)
 
         ident_b = keep.tile([P, P], BF16, name="ident_b")
         make_identity(nc, ident_b[:])
@@ -127,11 +127,22 @@ def tile_middlelayer_w_kernel(tc, in_data, W_words, W_scales, bias, out):
 
         a1 = keep.tile([P, H], F32, name="a1")
         pending = []
+
+        def store_pending():
+            for js in pending:
+                nc.sync.dma_start(
+                    out=out_rows[:, 2 * js : 2 * (js + BANK)],
+                    in_=out_sb[:, js : js + BANK, :].rearrange("p j e -> p (j e)"),
+                )
+            pending.clear()
+
         i = 0
         for r, (c0, nb, gs) in enumerate(ROUNDS):
             accs = [psum.tile([P, BANK], F32, tag="bank", name="acc%d" % (c0 + j)) for j in range(nb)]
             for g0 in range(0, G, gs):
                 load_w(i + AHEAD)
+                if i + AHEAD == len(chunks) - 1:
+                    store_pending()
                 w = w_tiles[i]
                 i += 1
                 for gi in range(gs):
@@ -169,9 +180,4 @@ def tile_middlelayer_w_kernel(tc, in_data, W_words, W_scales, bias, out):
                     )
                     pending.append(j0)
                     if i + AHEAD >= len(chunks):
-                        for js in pending:
-                            nc.sync.dma_start(
-                                out=out_rows[:, 2 * js : 2 * (js + BANK)],
-                                in_=out_sb[:, js : js + BANK, :].rearrange("p j e -> p (j e)"),
-                            )
-                        pending = []
+                        store_pending()

@@ -17,12 +17,13 @@ G = K // 512
 N = 6144
 H = N // 2
 BANK = 512
+HALF = BANK // 2
 HB = H // BANK
 
 FLOPS = 2 * B * K * N
 
-ROUNDS = ((0, 6, 1), (6, 3, 1), (9, 2, 1), (11, 1, 2))
-W_BUFS = 10
+ROUNDS = ((0, 8, 1), (8, 3, 1), (11, 1, 2))
+W_BUFS = 7
 AHEAD = W_BUFS - 1
 
 
@@ -129,10 +130,12 @@ def tile_middlelayer_w_kernel(tc, in_data, W_words, W_scales, bias, out):
         pending = []
 
         def store_pending():
-            for js in pending:
+            if pending:
+                js = pending[0]
+                je = pending[-1] + BANK
                 nc.sync.dma_start(
-                    out=out_rows[:, 2 * js : 2 * (js + BANK)],
-                    in_=out_sb[:, js : js + BANK, :].rearrange("p j e -> p (j e)"),
+                    out=out_rows[:, 2 * js : 2 * je],
+                    in_=out_sb[:, js:je, :].rearrange("p j e -> p (j e)"),
                 )
             pending.clear()
 
@@ -167,17 +170,28 @@ def tile_middlelayer_w_kernel(tc, in_data, W_words, W_scales, bias, out):
                 else:
                     j0 = BANK * (c - HB)
                     nt = tmp.tile([P, BANK], F32, name="nt")
+                    for u in range(2):
+                        nc.vector.scalar_tensor_tensor(
+                            out=nt[:, HALF * u : HALF * (u + 1)],
+                            in0=accs[j][:, HALF * u : HALF * (u + 1)],
+                            scalar=-1.0,
+                            in1=bias_bc[:, BANK * c + HALF * u : BANK * c + HALF * (u + 1)],
+                            op0=ALU.mult,
+                            op1=ALU.subtract,
+                        )
+                    rh = tmp.tile([P, HALF], F32, name="rh")
                     nc.vector.scalar_tensor_tensor(
-                        out=nt[:], in0=accs[j][:], scalar=-1.0, in1=bias_bc[:, cols], op0=ALU.mult, op1=ALU.subtract
+                        out=rh[:], in0=nt[:, 0:HALF], scalar=0.0, in1=a1[:, j0 : j0 + HALF], op0=ALU.min, op1=ALU.add
                     )
                     nc.vector.scalar_tensor_tensor(
-                        out=out_sb[:, j0 : j0 + BANK, 0],
-                        in0=nt[:],
+                        out=out_sb[:, j0 + HALF : j0 + BANK, 0],
+                        in0=nt[:, HALF:BANK],
                         scalar=0.0,
-                        in1=a1[:, j0 : j0 + BANK],
+                        in1=a1[:, j0 + HALF : j0 + BANK],
                         op0=ALU.min,
                         op1=ALU.add,
                     )
+                    nc.scalar.copy(out=out_sb[:, j0 : j0 + HALF, 0], in_=rh[:])
                     pending.append(j0)
                     if i + AHEAD >= len(chunks):
                         store_pending()

@@ -54,11 +54,12 @@ def tile_middlelayer_w_kernel(tc, in_data, W_words, W_scales, bias, out):
         nc.scalar.dma_start(out=bias_rows[8:12, :], in_=bias_by_bank[8:12, :])
 
         for h in range(2):
-            for q in (0, 2, 1, 3):
-                nc.gpsimd.dma_start(
-                    out=planes[32 * q : 32 * q + 16, h, :].bitcast(F32),
-                    in_=W_scales[4 * h : 4 * h + 4, 4 * q : 4 * q + 4, :].bitcast(F32),
-                )
+            for s in range(2):
+                for q in range(4):
+                    nc.sync.dma_start(
+                        out=planes[32 * q : 32 * q + 16, h, H * s : H * (s + 1)].bitcast(I32),
+                        in_=W_scales[4 * h : 4 * h + 4, 4 * q : 4 * q + 4, H * s : H * (s + 1)].bitcast(I32),
+                    )
 
         chunks = []
         for r, (c0, nb, gs) in enumerate(ROUNDS):

@@ -53,13 +53,14 @@ def tile_middlelayer_w_kernel(tc, in_data, W_words, W_scales, bias, out):
         nc.scalar.dma_start(out=bias_rows[0:8, :], in_=bias_by_bank[0:8, :])
         nc.scalar.dma_start(out=bias_rows[8:12, :], in_=bias_by_bank[8:12, :])
 
-        for h in range(2):
-            for s in range(2):
-                for q in range(4):
-                    nc.sync.dma_start(
-                        out=planes[32 * q : 32 * q + 16, h, H * s : H * (s + 1)].bitcast(I32),
-                        in_=W_scales[4 * h : 4 * h + 4, 4 * q : 4 * q + 4, H * s : H * (s + 1)].bitcast(I32),
-                    )
+        for qs in ((2, 3), (0, 1)):
+            for h in range(2):
+                for s in range(2):
+                    for q in qs:
+                        nc.sync.dma_start(
+                            out=planes[32 * q : 32 * q + 16, h, H * s : H * (s + 1)].bitcast(I32),
+                            in_=W_scales[4 * h : 4 * h + 4, 4 * q : 4 * q + 4, H * s : H * (s + 1)].bitcast(I32),
+                        )
 
         chunks = []
         for r, (c0, nb, gs) in enumerate(ROUNDS):

@@ -18,6 +18,7 @@ N = 6144
 H = N // 2
 BANK = 512
 HALF = BANK // 2
+SC_COLS = 384
 HB = H // BANK
 
 FLOPS = 2 * B * K * N
@@ -172,28 +173,29 @@ def tile_middlelayer_w_kernel(tc, in_data, W_words, W_scales, bias, out):
                 else:
                     j0 = BANK * (c - HB)
                     nt = tmp.tile([P, BANK], F32, name="nt")
-                    for u in range(2):
+                    sc = HALF if c == N // BANK - 1 else SC_COLS
+                    rh = tmp.tile([P, sc], F32, name="rh")
+                    for lo, hi in ((0, sc), (sc, BANK)):
                         nc.vector.scalar_tensor_tensor(
-                            out=nt[:, HALF * u : HALF * (u + 1)],
-                            in0=accs[j][:, HALF * u : HALF * (u + 1)],
+                            out=nt[:, lo:hi],
+                            in0=accs[j][:, lo:hi],
                             scalar=-1.0,
-                            in1=bias_bc[:, BANK * c + HALF * u : BANK * c + HALF * (u + 1)],
+                            in1=bias_bc[:, BANK * c + lo : BANK * c + hi],
                             op0=ALU.mult,
                             op1=ALU.subtract,
                         )
-                    rh = tmp.tile([P, HALF], F32, name="rh")
                     nc.vector.scalar_tensor_tensor(
-                        out=rh[:], in0=nt[:, 0:HALF], scalar=0.0, in1=a1[:, j0 : j0 + HALF], op0=ALU.min, op1=ALU.add
+                        out=rh[:], in0=nt[:, 0:sc], scalar=0.0, in1=a1[:, j0 : j0 + sc], op0=ALU.min, op1=ALU.add
                     )
                     nc.vector.scalar_tensor_tensor(
-                        out=out_sb[:, j0 + HALF : j0 + BANK, 0],
-                        in0=nt[:, HALF:BANK],
+                        out=out_sb[:, j0 + sc : j0 + BANK, 0],
+                        in0=nt[:, sc:BANK],
                         scalar=0.0,
-                        in1=a1[:, j0 + HALF : j0 + BANK],
+                        in1=a1[:, j0 + sc : j0 + BANK],
                         op0=ALU.min,
                         op1=ALU.add,
                     )
-                    nc.scalar.copy(out=out_sb[:, j0 : j0 + HALF, 0], in_=rh[:])
+                    nc.scalar.copy(out=out_sb[:, j0 : j0 + sc, 0], in_=rh[:])
                     pending.append(j0)
                     if i + AHEAD >= len(chunks):
                         store_pending()

@@ -49,18 +49,17 @@ def tile_middlelayer_w_kernel(tc, in_data, W_words, W_scales, bias, out):
         make_identity(nc, ident_f[:])
 
         x_raw = keep.tile([P, 2 * K], BF16, name="x_raw")
-        for i in range(2):
-            nc.sync.dma_start(out=x_raw[:, K * i : K * (i + 1)], in_=in_data[:, K * i : K * (i + 1)])
+        nc.sync.dma_start(out=x_raw[:], in_=in_data)
         nc.scalar.dma_start(out=bias_rows[0:8, :], in_=bias_by_bank[0:8, :])
         nc.scalar.dma_start(out=bias_rows[8:12, :], in_=bias_by_bank[8:12, :])
 
-        for qs in ((2, 3), (0, 1)):
+        for qs, width in (((2, 3), N), ((0, 1), H)):
             for h in range(2):
-                for s in range(2):
+                for n0 in range(0, N, width):
                     for q in qs:
                         nc.sync.dma_start(
-                            out=planes[32 * q : 32 * q + 16, h, H * s : H * (s + 1)].bitcast(I32),
-                            in_=W_scales[4 * h : 4 * h + 4, 4 * q : 4 * q + 4, H * s : H * (s + 1)].bitcast(I32),
+                            out=planes[32 * q : 32 * q + 16, h, n0 : n0 + width].bitcast(I32),
+                            in_=W_scales[4 * h : 4 * h + 4, 4 * q : 4 * q + 4, n0 : n0 + width].bitcast(I32),
                         )
 
         chunks = []

@@ -23,8 +23,12 @@ HB = H // BANK
 
 FLOPS = 2 * B * K * N
 
-ROUNDS = ((0, 8, 1), (8, 3, 1), (11, 1, 2))
-W_BUFS = 7
+ROUNDS = (
+    (0, 8, ((0, 1), (2, 3), (4, 5), (6,), (7,))),
+    (8, 3, ((0, 1), (2, 3), (4, 5), (6,), (7,))),
+    (11, 1, ((0, 1, 2, 3), (4, 5), (6, 7))),
+)
+W_BUFS = 4
 AHEAD = W_BUFS - 1
 
 
@@ -39,6 +43,7 @@ def tile_middlelayer_w_kernel(tc, in_data, W_words, W_scales, bias, out):
         planes = keep.tile([P, 2, N], U8, name="planes", align_bytes=64)
         bias_rows = keep.tile([P, BANK], BF16, name="bias_rows")
         out_sb = keep.tile([P, H, 2], F32, name="out_sb")
+        x_raw = out_sb[:].rearrange("p j e -> p (j e)")[:, 0:K].bitcast(BF16)
         nc.vector.memset(bias_rows[:], 0.0)
         nc.vector.memset(planes[:, 0, :].bitcast(I32), 0)
         nc.vector.memset(planes[:, 1, :].bitcast(I32), 0)
@@ -48,8 +53,7 @@ def tile_middlelayer_w_kernel(tc, in_data, W_words, W_scales, bias, out):
         ident_f = keep.tile([P, P], F32, name="ident_f")
         make_identity(nc, ident_f[:])
 
-        x_raw = keep.tile([P, 2 * K], BF16, name="x_raw")
-        nc.sync.dma_start(out=x_raw[:], in_=in_data)
+        nc.sync.dma_start(out=x_raw, in_=in_data)
         nc.scalar.dma_start(out=bias_rows[0:8, :], in_=bias_by_bank[0:8, :])
         nc.scalar.dma_start(out=bias_rows[8:12, :], in_=bias_by_bank[8:12, :])
 
@@ -62,19 +66,15 @@ def tile_middlelayer_w_kernel(tc, in_data, W_words, W_scales, bias, out):
                             in_=W_scales[4 * h : 4 * h + 4, 4 * q : 4 * q + 4, n0 : n0 + width].bitcast(I32),
                         )
 
-        chunks = []
-        for r, (c0, nb, gs) in enumerate(ROUNDS):
-            for g0 in range(0, G, gs):
-                chunks.append((r, g0, gs))
+        chunks = [(c0, nb, gs) for c0, nb, loads in ROUNDS for gs in loads]
         w_tiles = {}
 
         def load_w(i):
             if i >= len(chunks):
                 return
-            r, g0, gs = chunks[i]
-            c0, nb, gs2 = ROUNDS[r]
-            w = wpool.tile([P, gs, nb * BANK], U32, tag="w", name="w", align_bytes=64)
-            src = W_words[g0 : g0 + gs].rearrange("g p n t -> p g (n t)")
+            c0, nb, gs = chunks[i]
+            w = wpool.tile([P, len(gs), nb * BANK], U32, tag="w", name="w", align_bytes=64)
+            src = W_words[gs[0] : gs[-1] + 1].rearrange("g p n t -> p g (n t)")
             nc.sync.dma_start(
                 out=w[:].bitcast(I32),
                 in_=src[:, :, 4 * BANK * c0 : 4 * BANK * (c0 + nb)].bitcast(I32),
@@ -100,7 +100,7 @@ def tile_middlelayer_w_kernel(tc, in_data, W_words, W_scales, bias, out):
             bbs.append(bb)
 
         x_sorted = keep.tile([P, G, 2, P], F32, name="x_sorted")
-        src_x = x_raw[:].rearrange("b (g p u e c) -> b g u p e c", g=G, p=P, u=2, e=2, c=2)
+        src_x = x_raw.rearrange("b (g p u e c) -> b g u p e c", g=G, p=P, u=2, e=2, c=2)
         dst_x = x_sorted[:].bitcast(BF16).rearrange("b g u (p e) -> b g u p e", e=2)
         for g in range(G):
             if g % 2 == 0:
@@ -142,16 +142,15 @@ def tile_middlelayer_w_kernel(tc, in_data, W_words, W_scales, bias, out):
             pending.clear()
 
         i = 0
-        for r, (c0, nb, gs) in enumerate(ROUNDS):
+        for c0, nb, loads in ROUNDS:
             accs = [psum.tile([P, BANK], F32, tag="bank", name="acc%d" % (c0 + j)) for j in range(nb)]
-            for g0 in range(0, G, gs):
+            for gs in loads:
                 load_w(i + AHEAD)
                 if i + AHEAD == len(chunks) - 1:
                     store_pending()
                 w = w_tiles[i]
                 i += 1
-                for gi in range(gs):
-                    g = g0 + gi
+                for gi, g in enumerate(gs):
                     for j in range(nb):
                         c = c0 + j
                         nc.tensor.matmul_mx(

@@ -26,7 +26,7 @@ FLOPS = 2 * B * K * N
 ROUNDS = (
     (0, 8, ((0, 1), (2, 3), (4, 5), (6,), (7,))),
     (8, 3, ((0, 1), (2, 3), (4, 5), (6,), (7,))),
-    (11, 1, ((0, 1, 2, 3), (4, 5), (6, 7))),
+    (11, 1, ((0, 1, 2, 3), (4, 5, 6, 7))),
 )
 W_BUFS = 4
 AHEAD = W_BUFS - 1
@@ -53,7 +53,7 @@ def tile_middlelayer_w_kernel(tc, in_data, W_words, W_scales, bias, out):
         ident_f = keep.tile([P, P], F32, name="ident_f")
         make_identity(nc, ident_f[:])
 
-        nc.sync.dma_start(out=x_raw, in_=in_data)
+        nc.scalar.dma_start(out=x_raw, in_=in_data)
         nc.scalar.dma_start(out=bias_rows[0:8, :], in_=bias_by_bank[0:8, :])
         nc.scalar.dma_start(out=bias_rows[8:12, :], in_=bias_by_bank[8:12, :])
 

import concourse.mybir as mybir
from concourse.masks import make_identity

F32 = mybir.dt.float32
BF16 = mybir.dt.bfloat16
I32 = mybir.dt.int32
U32 = mybir.dt.uint32
U8 = mybir.dt.uint8
FP8X4 = mybir.dt.float8_e4m3fn_x4
ALU = mybir.AluOpType
ACT = mybir.ActivationFunctionType

P = 128
B = 128
K = 4096
G = K // 512
N = 6144
H = N // 2
BANK = 512
HALF = BANK // 2
SC_COLS = 384
HB = H // BANK

FLOPS = 2 * B * K * N

ROUNDS = (
    (0, 8, ((0, 1), (2, 3), (4, 5), (6,), (7,))),
    (8, 3, ((0, 1), (2, 3), (4, 5), (6,), (7,))),
    (11, 1, ((0, 1, 2, 3), (4, 5, 6, 7))),
)
W_BUFS = 4
AHEAD = W_BUFS - 1


def tile_middlelayer_w_kernel(tc, in_data, W_words, W_scales, bias, out):
    nc = tc.nc
    out_rows = out.rearrange("b n o -> b (n o)")
    bias_by_bank = bias.rearrange("(r c) -> r c", c=BANK)

    with tc.tile_pool(name="keep", bufs=1) as keep, tc.tile_pool(name="wpool", bufs=W_BUFS) as wpool, tc.tile_pool(
        name="tmp", bufs=3
    ) as tmp, tc.psum_pool(name="psum", bufs=8) as psum, tc.manual_schedule():
        planes = keep.tile([P, 2, N], U8, name="planes", align_bytes=64)
        bias_rows = keep.tile([P, BANK], BF16, name="bias_rows")
        out_sb = keep.tile([P, H, 2], F32, name="out_sb")
        x_raw = out_sb[:].rearrange("p j e -> p (j e)")[:, 0:K].bitcast(BF16)
        nc.vector.memset(bias_rows[:], 0.0)
        nc.vector.memset(planes[:, 0, :].bitcast(I32), 0)
        nc.vector.memset(planes[:, 1, :].bitcast(I32), 0)

        ident_b = keep.tile([P, P], BF16, name="ident_b")
        make_identity(nc, ident_b[:])
        ident_f = keep.tile([P, P], F32, name="ident_f")
        make_identity(nc, ident_f[:])

        nc.scalar.dma_start(out=x_raw, in_=in_data)
        nc.scalar.dma_start(out=bias_rows[0:8, :], in_=bias_by_bank[0:8, :])
        nc.scalar.dma_start(out=bias_rows[8:12, :], in_=bias_by_bank[8:12, :])

        for qs, width in (((2, 3), N), ((0, 1), H)):
            for h in range(2):
                for n0 in range(0, N, width):
                    for q in qs:
                        nc.sync.dma_start(
                            out=planes[32 * q : 32 * q + 16, h, n0 : n0 + width].bitcast(I32),
                            in_=W_scales[4 * h : 4 * h + 4, 4 * q : 4 * q + 4, n0 : n0 + width].bitcast(I32),
                        )

        chunks = [(c0, nb, gs) for c0, nb, loads in ROUNDS for gs in loads]
        w_tiles = {}

        def load_w(i):
            if i >= len(chunks):
                return
            c0, nb, gs = chunks[i]
            w = wpool.tile([P, len(gs), nb * BANK], U32, tag="w", name="w", align_bytes=64)
            src = W_words[gs[0] : gs[-1] + 1].rearrange("g p n t -> p g (n t)")
            nc.sync.dma_start(
                out=w[:].bitcast(I32),
                in_=src[:, :, 4 * BANK * c0 : 4 * BANK * (c0 + nb)].bitcast(I32),
            )
            w_tiles[i] = w

        for i in range(AHEAD):
            load_w(i)

        bias_bc = keep.tile([P, N], BF16, name="bias_bc")
        bbs = []
        for i in range(N // (2 * BANK)):
            bb = psum.tile([P, 2 * BANK], BF16, tag="bank", name="bb")
            for s in range(2):
                c = 2 * i + s
                nc.tensor.matmul(
                    bb[:, BANK * s : BANK * (s + 1)],
                    lhsT=ident_b[:, c : c + 1].to_broadcast([P, P]),
                    rhs=bias_rows[:],
                    start=True,
                    stop=True,
                )
            bbs.append(bb)

        x_sorted = keep.tile([P, G, 2, P], F32, name="x_sorted")
        src_x = x_raw.rearrange("b (g p u e c) -> b g u p e c", g=G, p=P, u=2, e=2, c=2)
        dst_x = x_sorted[:].bitcast(BF16).rearrange("b g u (p e) -> b g u p e", e=2)
        for g in range(G):
            if g % 2 == 0:
                nc.vector.tensor_copy(out=dst_x[:, g, :, :, :], in_=src_x[:, g, :, :, :, 1])
            else:
                nc.scalar.copy(out=dst_x[:, g, :, :, :], in_=src_x[:, g, :, :, :, 1])
        for i, bb in enumerate(bbs):
            nc.scalar.copy(out=bias_bc[:, 2 * BANK * i : 2 * BANK * (i + 1)], in_=bb[:])

        grouped = keep.tile([P, G, 4 * B], BF16, name="grouped", align_bytes=64)
        grouped_w = grouped[:].bitcast(F32).rearrange("p g (b u) -> p g b u", u=2)
        x_codes = keep.tile([P, G * B], U32, name="x_codes", align_bytes=64)
        x_planes = keep.tile([P, G * B], U8, name="x_planes", align_bytes=64)
        for i in range(4):
            xt = psum.tile([P, 2, 2, B], F32, tag="bank", name="xt")
            for gg in range(2):
                for u in range(2):
                    nc.tensor.transpose(xt[:, gg, u, :], x_sorted[:, 2 * i + gg, u, :], ident_f[:])
            nc.vector.tensor_copy(out=grouped_w[:, 2 * i : 2 * i + 2, :, :], in_=xt[:].rearrange("p g u b -> p g b u"))
        for i in range(4):
            nc.vector.quantize_mx(
                out=x_codes[:, 2 * B * i : 2 * B * (i + 1)].bitcast(FP8X4),
                scales=x_planes[:, 2 * B * i : 2 * B * (i + 1)],
                in_=grouped[:, 2 * i : 2 * i + 2, :].rearrange("p g c -> p (g c)"),
            )
        nc.vector.memset(out_sb[:], 0.0)

        a1 = keep.tile([P, H], F32, name="a1")
        pending = []

        def store_pending():
            if pending:
                js = pending[0]
                je = pending[-1] + BANK
                nc.sync.dma_start(
                    out=out_rows[:, 2 * js : 2 * je],
                    in_=out_sb[:, js:je, :].rearrange("p j e -> p (j e)"),
                )
            pending.clear()

        i = 0
        for c0, nb, loads in ROUNDS:
            accs = [psum.tile([P, BANK], F32, tag="bank", name="acc%d" % (c0 + j)) for j in range(nb)]
            for gs in loads:
                load_w(i + AHEAD)
                if i + AHEAD == len(chunks) - 1:
                    store_pending()
                w = w_tiles[i]
                i += 1
                for gi, g in enumerate(gs):
                    for j in range(nb):
                        c = c0 + j
                        nc.tensor.matmul_mx(
                            out=accs[j][:],
                            lhsT=x_codes[:, B * g : B * (g + 1)].bitcast(FP8X4),
                            lhsT_scale=x_planes[:, B * g : B * (g + 1)],
                            rhs=w[:, gi, BANK * j : BANK * (j + 1)].bitcast(FP8X4),
                            rhs_scale=planes[4 * (g % 4) : P, g // 4, BANK * c : BANK * (c + 1)],
                            start=(g == 0),
                            stop=(g == G - 1),
                        )
            for j in range(nb):
                c = c0 + j
                cols = slice(BANK * c, BANK * (c + 1))
                if c < HB:
                    nc.vector.tensor_tensor(out=a1[:, cols], in0=accs[j][:], in1=bias_bc[:, cols], op=ALU.add)
                    nc.scalar.activation(out=a1[:, cols], in_=a1[:, cols], func=ACT.Relu)
                else:
                    j0 = BANK * (c - HB)
                    nt = tmp.tile([P, BANK], F32, name="nt")
                    sc = HALF if c == N // BANK - 1 else SC_COLS
                    rh = tmp.tile([P, sc], F32, name="rh")
                    for lo, hi in ((0, sc), (sc, BANK)):
                        nc.vector.scalar_tensor_tensor(
                            out=nt[:, lo:hi],
                            in0=accs[j][:, lo:hi],
                            scalar=-1.0,
                            in1=bias_bc[:, BANK * c + lo : BANK * c + hi],
                            op0=ALU.mult,
                            op1=ALU.subtract,
                        )
                    nc.vector.scalar_tensor_tensor(
                        out=rh[:], in0=nt[:, 0:sc], scalar=0.0, in1=a1[:, j0 : j0 + sc], op0=ALU.min, op1=ALU.add
                    )
                    nc.vector.scalar_tensor_tensor(
                        out=out_sb[:, j0 + sc : j0 + BANK, 0],
                        in0=nt[:, sc:BANK],
                        scalar=0.0,
                        in1=a1[:, j0 + sc : j0 + BANK],
                        op0=ALU.min,
                        op1=ALU.add,
                    )
                    nc.scalar.copy(out=out_sb[:, j0 : j0 + sc, 0], in_=rh[:])
                    pending.append(j0)
                    if i + AHEAD >= len(chunks):
                        store_pending()
